import numpy as np
import ml_dtypes


def mxq(x, axis, fmt="e4m3"):
    dtype, down = {"e4m3": (ml_dtypes.float8_e4m3fn, 7), "e5m2": (ml_dtypes.float8_e5m2, 14)}[fmt]
    v = np.moveaxis(np.asarray(x, np.float32).astype(ml_dtypes.bfloat16).astype(np.float64), axis, -1)
    blocks = v.reshape(v.shape[:-1] + (-1, 32))
    amax = np.abs(blocks).max(-1, keepdims=True)
    byte = np.maximum(np.where(amax > 0, np.frexp(amax)[1] - 1 + 127, 0) - down, 1)
    scale = np.exp2(byte - 127.0)
    codes = (blocks / scale).astype(np.float32).astype(dtype).astype(np.float64)
    return np.moveaxis((codes * scale).reshape(v.shape), -1, axis)


WIDE = False


def mx_kscale(k):
    if not WIDE:
        return np.ones(k)
    levels = np.array([10, -10, 5, -5, 0])
    a = np.random.permutation(np.resize(levels, k // 512 * 4)).reshape(k // 512, 4)
    idx = np.arange(k)
    return np.exp2(a[idx // 512, idx % 128 // 32])


BF16 = ml_dtypes.bfloat16


def bf(x):
    return np.asarray(x, np.float32).astype(BF16)


def f64(x):
    return np.asarray(x).astype(np.float64)


B, C, L = 4, 1024, 1024
BETA_MIN = 1e-06
PEDESTAL = (2.0 ** -18) ** 2


def nn_reparam(p, minimum):
    bound = (minimum + PEDESTAL) ** 0.5
    return np.maximum(p, bound) ** 2 - PEDESTAL


def setup_inputs():
    t = np.exp2(np.round(np.log2(mx_kscale(C)) / 2))
    amp = np.exp2(np.random.uniform(-1.0, 1.0, (B, 1, L)))
    return {"x": bf(np.random.standard_normal((B, C, L)) * amp * t[None, :, None]),
            "beta_param": bf(np.random.standard_normal(C) * t),
            "gamma_param": bf(np.random.standard_normal((C, C)) * np.sqrt(2.0 / C) * t[:, None] / t[None, :])}


def reference(x, beta_param, gamma_param):
    x = f64(x)
    beta = nn_reparam(f64(beta_param), BETA_MIN)
    gamma = nn_reparam(f64(gamma_param), 0.0)
    norm = (mxq(gamma, 1, "e4m3") @ mxq(x * x, 1, "e4m3")) + beta[None, :, None]
    return x * (1.0 / np.sqrt(norm))

@@ -1,0 +1,154 @@
+from contextlib import ExitStack
+
+import concourse.mybir as mybir
+from concourse.masks import make_identity
+
+F32 = mybir.dt.float32
+BF16 = mybir.dt.bfloat16
+U32 = mybir.dt.uint32
+U8 = mybir.dt.uint8
+FP8X4 = mybir.dt.float8_e4m3fn_x4
+ACT = mybir.ActivationFunctionType
+ALU = mybir.AluOpType
+
+P = 128
+B, C, L = 4, 1024, 1024
+HALF = 512
+A = 2.0 ** -18
+PEDESTAL = 2.0 ** -36
+BETA_BOUND = (1e-06 + PEDESTAL) ** 0.5
+WS = 352
+
+FLOPS = 2 * B * C * C * L
+
+
+def tile_gdn_1d_t_kernel(tc, x, beta_param, gamma_param, out):
+    nc = tc.nc
+    with ExitStack() as ctx:
+        keep = ctx.enter_context(tc.tile_pool(name="keep", bufs=1))
+        upool = ctx.enter_context(tc.tile_pool(name="upool", bufs=2))
+        sqpool = ctx.enter_context(tc.tile_pool(name="sqpool", bufs=3))
+        rpool = ctx.enter_context(tc.tile_pool(name="rpool", bufs=4))
+        opool = ctx.enter_context(tc.tile_pool(name="opool", bufs=4))
+        psum = ctx.enter_context(tc.psum_pool(name="psum", bufs=8))
+
+        ident = keep.tile([P, P], F32, name="ident")
+        make_identity(nc, ident[:])
+
+        gp = keep.tile([P, 8 * C], BF16, name="gp")
+        gview = gamma_param.rearrange("(c p j) i -> c p j i", c=2, j=4)
+        for c in range(2):
+            nc.sync.dma_start(
+                out=gp[:, c * 4 * C : (c + 1) * 4 * C].rearrange("p (j i) -> p j i", j=4),
+                in_=gview[c],
+            )
+        bp = keep.tile([P, 2, 4], BF16, name="bp")
+        nc.sync.dma_start(out=bp[:], in_=beta_param.rearrange("(c p j) -> p c j", c=2, j=4))
+        xs = []
+        for b in range(B):
+            xb = keep.tile([P, 8, L], BF16, name="x%d" % b)
+            xview = x[b].rearrange("(c p j) l -> c p j l", c=2, j=4)
+            for c in range(2):
+                nc.sync.dma_start(out=xb[:, 4 * c : 4 * c + 4, :], in_=xview[c])
+            xs.append(xb)
+
+        bt = keep.tile([P, 8], F32, name="bt")
+        nc.vector.tensor_scalar_max(out=bt[:], in0=bp[:].rearrange("p c j -> p (c j)"), scalar1=BETA_BOUND)
+        bsq = keep.tile([P, 8], F32, name="bsq")
+        nc.vector.tensor_tensor(out=bsq[:], in0=bt[:], in1=bt[:], op=ALU.mult)
+        beta = keep.tile([P, 8], F32, name="beta")
+        nc.vector.tensor_scalar_add(out=beta[:], in0=bsq[:], scalar1=-PEDESTAL)
+
+        gw = gp[:].bitcast(F32)
+        g_bf = keep.tile([P, 2, 4096], BF16, name="g_bf", align_bytes=64)
+        g_codes = keep.tile([P, 2, 1024], U32, name="g_codes", align_bytes=64)
+        g_scales = keep.tile([P, 2, 1024], U8, name="g_scales", align_bytes=64)
+        for c in range(2):
+            for cp in range(2):
+                u = upool.tile([P, 4, 512], F32, name="u")
+                for half in range(2):
+                    bank = psum.tile([P, HALF], F32, name="bank", tag="bank")
+                    for g in range(2):
+                        cj = 4 * c + 2 * half + g
+                        words = gw[:, cj * 512 + 256 * cp : cj * 512 + 256 * cp + 256].rearrange(
+                            "p (q u) -> p u q", u=2
+                        )
+                        for uu in range(2):
+                            col = (2 * g + uu) * P
+                            nc.tensor.transpose(bank[:, col : col + P], words[:, uu, :], ident[:])
+                    bank_bf = bank[:].bitcast(BF16)
+                    for g in range(2):
+                        nc.scalar.activation(
+                            out=u[:, 2 * half + g, :].rearrange("q (m u e) -> q m u e", u=2, e=2),
+                            in_=bank_bf[:, g * 512 : (g + 1) * 512].rearrange("q (u m e) -> q m u e", u=2, e=2),
+                            func=ACT.Relu,
+                            bias=-A,
+                            scale=1.0,
+                        )
+                uf = u[:].rearrange("q j n -> q (j n)")
+                nc.vector.scalar_tensor_tensor(
+                    out=g_bf[:, cp, c * 2048 : (c + 1) * 2048],
+                    in0=uf,
+                    scalar=2.0 * A,
+                    in1=uf,
+                    op0=ALU.add,
+                    op1=ALU.mult,
+                )
+                nc.vector.quantize_mx(
+                    out=g_codes[:, cp, c * 512 : (c + 1) * 512].bitcast(FP8X4),
+                    scales=g_scales[:, cp, c * 512 : (c + 1) * 512],
+                    in_=g_bf[:, cp, c * 2048 : (c + 1) * 2048],
+                )
+
+        x_codes = []
+        x_scales = []
+        for b in range(B):
+            x_codes.append(keep.tile([P, 2, L], U32, name="xc%d" % b, align_bytes=64))
+            x_scales.append(keep.tile([P, 2, L], U8, name="xsc%d" % b, align_bytes=64))
+
+        def square_and_quantise(b, cp, h):
+            cols = slice(h * HALF, (h + 1) * HALF)
+            xg = sqpool.tile([P, HALF, 4], BF16, name="xg", align_bytes=64)
+            src = xs[b][:, 4 * cp : 4 * cp + 4, cols].rearrange("p t (c i) -> p c t i", i=4)
+            dst = xg[:].rearrange("p (c i) t -> p c t i", i=4)
+            cs = WS // 4
+            nc.scalar.activation(out=dst[:, :cs], in_=src[:, :cs], func=ACT.Square)
+            nc.vector.tensor_tensor(out=dst[:, cs:], in0=src[:, cs:], in1=src[:, cs:], op=ALU.mult)
+            nc.vector.quantize_mx(
+                out=x_codes[b][:, cp, cols].bitcast(FP8X4),
+                scales=x_scales[b][:, cp, cols],
+                in_=xg[:].rearrange("p w t -> p (w t)"),
+            )
+
+        def normalise(b, cj):
+            oview = out[b].rearrange("(c p j) l -> c j p l", c=2, j=4)
+            o = opool.tile([P, L], F32, name="o")
+            for h in range(2):
+                cols = slice(h * HALF, (h + 1) * HALF)
+                acc = psum.tile([P, HALF], F32, name="acc", tag="bank")
+                for cp in range(2):
+                    nc.tensor.matmul_mx(
+                        out=acc[:],
+                        lhsT=g_codes[:, cp, cj * P : (cj + 1) * P].bitcast(FP8X4),
+                        lhsT_scale=g_scales[:, cp, cj * P : (cj + 1) * P],
+                        rhs=x_codes[b][:, cp, cols].bitcast(FP8X4),
+                        rhs_scale=x_scales[b][:, cp, cols],
+                        start=(cp == 0),
+                        stop=(cp == 1),
+                    )
+                r = rpool.tile([P, HALF], F32, name="r")
+                nc.scalar.activation(
+                    out=r[:], in_=acc[:], func=ACT.Abs_reciprocal_sqrt, bias=beta[:, cj : cj + 1], scale=1.0
+                )
+                nc.vector.tensor_tensor(out=o[:, cols], in0=xs[b][:, cj, cols], in1=r[:], op=ALU.mult)
+            nc.sync.dma_start(out=oview[cj // 4, cj % 4], in_=o[:])
+
+        units = [(cp, h) for h in range(2) for cp in range(2)]
+        for cp, h in units:
+            square_and_quantise(0, cp, h)
+        for b in range(B):
+            for g in range(4):
+                normalise(b, 2 * g)
+                normalise(b, 2 * g + 1)
+                if b + 1 < B:
+                    square_and_quantise(b + 1, units[g][0], units[g][1])

@@ -17,7 +17,8 @@ HALF = 512
 A = 2.0 ** -18
 PEDESTAL = 2.0 ** -36
 BETA_BOUND = (1e-06 + PEDESTAL) ** 0.5
-WS = 352
+WS = 320
+SPLIT_ROWS = 2
 
 FLOPS = 2 * B * C * C * L
 
@@ -26,31 +27,43 @@ def tile_gdn_1d_t_kernel(tc, x, beta_param, gamma_param, out):
     nc = tc.nc
     with ExitStack() as ctx:
         keep = ctx.enter_context(tc.tile_pool(name="keep", bufs=1))
-        upool = ctx.enter_context(tc.tile_pool(name="upool", bufs=2))
+        sqf = ctx.enter_context(tc.tile_pool(name="sqf", bufs=2))
+        gbf = ctx.enter_context(tc.tile_pool(name="gbf", bufs=2))
         sqpool = ctx.enter_context(tc.tile_pool(name="sqpool", bufs=3))
-        rpool = ctx.enter_context(tc.tile_pool(name="rpool", bufs=4))
+        rpool = ctx.enter_context(tc.tile_pool(name="rpool", bufs=3))
         opool = ctx.enter_context(tc.tile_pool(name="opool", bufs=4))
         psum = ctx.enter_context(tc.psum_pool(name="psum", bufs=8))
+
+        one = keep.tile([P, 1], F32, name="one")
+        nc.vector.memset(one[:], 1.0)
+        warm = keep.tile([P, 1], F32, name="warm")
+        nc.scalar.activation(out=warm[:], in_=one[:], func=ACT.Abs_reciprocal_sqrt)
 
         ident = keep.tile([P, P], F32, name="ident")
         make_identity(nc, ident[:])
 
-        gp = keep.tile([P, 8 * C], BF16, name="gp")
-        gview = gamma_param.rearrange("(c p j) i -> c p j i", c=2, j=4)
-        for c in range(2):
-            nc.sync.dma_start(
-                out=gp[:, c * 4 * C : (c + 1) * 4 * C].rearrange("p (j i) -> p j i", j=4),
-                in_=gview[c],
-            )
         bp = keep.tile([P, 2, 4], BF16, name="bp")
-        nc.sync.dma_start(out=bp[:], in_=beta_param.rearrange("(c p j) -> p c j", c=2, j=4))
-        xs = []
-        for b in range(B):
-            xb = keep.tile([P, 8, L], BF16, name="x%d" % b)
+        nc.scalar.dma_start(out=bp[:], in_=beta_param.rearrange("(c p j) -> p c j", c=2, j=4))
+        gview = gamma_param.rearrange("(c p j) i -> c p j i", c=2, j=4)
+        gp = [keep.tile([P, 2, C], BF16, name="gp%d" % q) for q in range(4)]
+        xs = [keep.tile([P, 8, L], BF16, name="x%d" % b) for b in range(B)]
+
+        def load_gamma(q):
+            j0 = 2 * (q % 2)
+            nc.sync.dma_start(out=gp[q][:], in_=gview[q // 2][:, j0 : j0 + 2, :])
+
+        def load_x(b, c):
             xview = x[b].rearrange("(c p j) l -> c p j l", c=2, j=4)
-            for c in range(2):
-                nc.sync.dma_start(out=xb[:, 4 * c : 4 * c + 4, :], in_=xview[c])
-            xs.append(xb)
+            nc.sync.dma_start(out=xs[b][:, 4 * c : 4 * c + 4, :], in_=xview[c])
+
+        load_gamma(0)
+        load_x(0, 0)
+        load_x(0, 1)
+        for q in range(1, 4):
+            load_gamma(q)
+        for b in range(1, B):
+            load_x(b, 0)
+            load_x(b, 1)
 
         bt = keep.tile([P, 8], F32, name="bt")
         nc.vector.tensor_scalar_max(out=bt[:], in0=bp[:].rearrange("p c j -> p (c j)"), scalar1=BETA_BOUND)
@@ -59,52 +72,39 @@ def tile_gdn_1d_t_kernel(tc, x, beta_param, gamma_param, out):
         beta = keep.tile([P, 8], F32, name="beta")
         nc.vector.tensor_scalar_add(out=beta[:], in0=bsq[:], scalar1=-PEDESTAL)
 
-        gw = gp[:].bitcast(F32)
-        g_bf = keep.tile([P, 2, 4096], BF16, name="g_bf", align_bytes=64)
-        g_codes = keep.tile([P, 2, 1024], U32, name="g_codes", align_bytes=64)
-        g_scales = keep.tile([P, 2, 1024], U8, name="g_scales", align_bytes=64)
-        for c in range(2):
-            for cp in range(2):
-                u = upool.tile([P, 4, 512], F32, name="u")
-                for half in range(2):
-                    bank = psum.tile([P, HALF], F32, name="bank", tag="bank")
-                    for g in range(2):
-                        cj = 4 * c + 2 * half + g
-                        words = gw[:, cj * 512 + 256 * cp : cj * 512 + 256 * cp + 256].rearrange(
-                            "p (q u) -> p u q", u=2
-                        )
-                        for uu in range(2):
-                            col = (2 * g + uu) * P
-                            nc.tensor.transpose(bank[:, col : col + P], words[:, uu, :], ident[:])
-                    bank_bf = bank[:].bitcast(BF16)
-                    for g in range(2):
-                        nc.scalar.activation(
-                            out=u[:, 2 * half + g, :].rearrange("q (m u e) -> q m u e", u=2, e=2),
-                            in_=bank_bf[:, g * 512 : (g + 1) * 512].rearrange("q (u m e) -> q m u e", u=2, e=2),
-                            func=ACT.Relu,
-                            bias=-A,
-                            scale=1.0,
-                        )
-                uf = u[:].rearrange("q j n -> q (j n)")
-                nc.vector.scalar_tensor_tensor(
-                    out=g_bf[:, cp, c * 2048 : (c + 1) * 2048],
-                    in0=uf,
-                    scalar=2.0 * A,
-                    in1=uf,
-                    op0=ALU.add,
-                    op1=ALU.mult,
-                )
-                nc.vector.quantize_mx(
-                    out=g_codes[:, cp, c * 512 : (c + 1) * 512].bitcast(FP8X4),
-                    scales=g_scales[:, cp, c * 512 : (c + 1) * 512],
-                    in_=g_bf[:, cp, c * 2048 : (c + 1) * 2048],
-                )
+        g_codes = keep.tile([P, 2048], U32, name="g_codes", align_bytes=64)
+        g_scales = keep.tile([P, 2048], U8, name="g_scales", align_bytes=64)
 
-        x_codes = []
-        x_scales = []
-        for b in range(B):
-            x_codes.append(keep.tile([P, 2, L], U32, name="xc%d" % b, align_bytes=64))
-            x_scales.append(keep.tile([P, 2, L], U8, name="xsc%d" % b, align_bytes=64))
+        def gamma_unit(q):
+            t = keep.tile([P, 2 * C], BF16, name="t%d" % q)
+            nc.vector.tensor_scalar_max(out=t[:], in0=gp[q][:].rearrange("p g i -> p (g i)"), scalar1=A)
+            tw = t[:].bitcast(F32)
+            sq = sqf.tile([P, 2, 2, 512], F32, name="sq")
+            for g in range(2):
+                bank = psum.tile([P, HALF], F32, name="bank", tag="bank")
+                for cp in range(2):
+                    w0 = g * 512 + 256 * cp
+                    words = tw[:, w0 : w0 + 256].rearrange("p (q u) -> p u q", u=2)
+                    for u in range(2):
+                        col = (2 * cp + u) * P
+                        nc.tensor.transpose(bank[:, col : col + P], words[:, u, :], ident[:])
+                bank_bf = bank[:].bitcast(BF16)
+                for cp in range(2):
+                    nc.scalar.activation(
+                        out=sq[:, g, cp, :].rearrange("q (m u e) -> q m u e", u=2, e=2),
+                        in_=bank_bf[:, cp * 512 : (cp + 1) * 512].rearrange("q (u m e) -> q m u e", u=2, e=2),
+                        func=ACT.Square,
+                    )
+            gb = gbf.tile([P, 2048], BF16, name="gb", align_bytes=64)
+            nc.vector.tensor_scalar_add(out=gb[:], in0=sq[:].rearrange("q g c n -> q (g c n)"), scalar1=-PEDESTAL)
+            nc.vector.quantize_mx(
+                out=g_codes[:, q * 512 : (q + 1) * 512].bitcast(FP8X4),
+                scales=g_scales[:, q * 512 : (q + 1) * 512],
+                in_=gb[:],
+            )
+
+        x_codes = [keep.tile([P, 2, L], U32, name="xc%d" % b, align_bytes=64) for b in range(B)]
+        x_scales = [keep.tile([P, 2, L], U8, name="xsc%d" % b, align_bytes=64) for b in range(B)]
 
         def square_and_quantise(b, cp, h):
             cols = slice(h * HALF, (h + 1) * HALF)
@@ -120,35 +120,43 @@ def tile_gdn_1d_t_kernel(tc, x, beta_param, gamma_param, out):
                 in_=xg[:].rearrange("p w t -> p (w t)"),
             )
 
-        def normalise(b, cj):
-            oview = out[b].rearrange("(c p j) l -> c j p l", c=2, j=4)
+        def normalise(b, cj, split):
+            oview = out[b].rearrange("(c p j) l -> c j p l", c=2, j=4)[cj // 4, cj % 4]
+            r = rpool.tile([P, L], F32, name="r")
             o = opool.tile([P, L], F32, name="o")
             for h in range(2):
                 cols = slice(h * HALF, (h + 1) * HALF)
                 acc = psum.tile([P, HALF], F32, name="acc", tag="bank")
                 for cp in range(2):
+                    w0 = cj * 256 + cp * P
                     nc.tensor.matmul_mx(
                         out=acc[:],
-                        lhsT=g_codes[:, cp, cj * P : (cj + 1) * P].bitcast(FP8X4),
-                        lhsT_scale=g_scales[:, cp, cj * P : (cj + 1) * P],
+                        lhsT=g_codes[:, w0 : w0 + P].bitcast(FP8X4),
+                        lhsT_scale=g_scales[:, w0 : w0 + P],
                         rhs=x_codes[b][:, cp, cols].bitcast(FP8X4),
                         rhs_scale=x_scales[b][:, cp, cols],
                         start=(cp == 0),
                         stop=(cp == 1),
                     )
-                r = rpool.tile([P, HALF], F32, name="r")
                 nc.scalar.activation(
-                    out=r[:], in_=acc[:], func=ACT.Abs_reciprocal_sqrt, bias=beta[:, cj : cj + 1], scale=1.0
+                    out=r[:, cols], in_=acc[:], func=ACT.Abs_reciprocal_sqrt, bias=beta[:, cj : cj + 1], scale=1.0
                 )
-                nc.vector.tensor_tensor(out=o[:, cols], in0=xs[b][:, cj, cols], in1=r[:], op=ALU.mult)
-            nc.sync.dma_start(out=oview[cj // 4, cj % 4], in_=o[:])
+                if split:
+                    nc.vector.tensor_tensor(out=o[:, cols], in0=xs[b][:, cj, cols], in1=r[:, cols], op=ALU.mult)
+                    nc.sync.dma_start(out=oview[:, cols], in_=o[:, cols])
+            if not split:
+                nc.vector.tensor_tensor(out=o[:], in0=xs[b][:, cj, :], in1=r[:], op=ALU.mult)
+                nc.sync.dma_start(out=oview, in_=o[:])
 
         units = [(cp, h) for h in range(2) for cp in range(2)]
+        gamma_unit(0)
         for cp, h in units:
             square_and_quantise(0, cp, h)
+        for q in range(1, 4):
+            gamma_unit(q)
         for b in range(B):
             for g in range(4):
-                normalise(b, 2 * g)
-                normalise(b, 2 * g + 1)
                 if b + 1 < B:
                     square_and_quantise(b + 1, units[g][0], units[g][1])
+                for cj in (2 * g, 2 * g + 1):
+                    normalise(b, cj, 8 * b + cj >= 8 * B - SPLIT_ROWS)

@@ -19,6 +19,8 @@ PEDESTAL = 2.0 ** -36
 BETA_BOUND = (1e-06 + PEDESTAL) ** 0.5
 WS = 320
 SPLIT_ROWS = 2
+SA = 256
+PSUM_X_BATCHES = 3
 
 FLOPS = 2 * B * C * C * L
 
@@ -41,6 +43,8 @@ def tile_gdn_1d_t_kernel(tc, x, beta_param, gamma_param, out):
 
         ident = keep.tile([P, P], F32, name="ident")
         make_identity(nc, ident[:])
+        ident_bf = keep.tile([P, P], BF16, name="ident_bf")
+        make_identity(nc, ident_bf[:])
 
         bp = keep.tile([P, 2, 4], BF16, name="bp")
         nc.scalar.dma_start(out=bp[:], in_=beta_param.rearrange("(c p j) -> p c j", c=2, j=4))
@@ -120,10 +124,45 @@ def tile_gdn_1d_t_kernel(tc, x, beta_param, gamma_param, out):
                 in_=xg[:].rearrange("p w t -> p (w t)"),
             )
 
+        GM = HALF - SA
+        shared = keep.tile([P, (2 * SA + GM) * 4], BF16, name="shared", align_bytes=64)
+
+        def square_shared(n, b, cp, h):
+            if n % 2 == 0:
+                base, s_tile, g_tile, s_pos, g_pos = 0, 0, SA, 0, SA
+            else:
+                base, s_tile, g_tile, s_pos, g_pos = SA, SA + GM, SA, GM, 0
+            rows = xs[b][:, 4 * cp : 4 * cp + 4, h * HALF : (h + 1) * HALF]
+            nc.scalar.activation(
+                out=shared[:, 4 * s_tile : 4 * (s_tile + SA)].rearrange("p (c i t) -> p c t i", i=4, t=4),
+                in_=rows[:, :, s_pos : s_pos + SA].rearrange("p t (c i) -> p c t i", i=4),
+                func=ACT.Square,
+            )
+            g_src = rows[:, :, g_pos : g_pos + GM].rearrange("p t l -> p l t")
+            nc.gpsimd.tensor_tensor(
+                out=shared[:, 4 * g_tile : 4 * (g_tile + GM)].rearrange("p (l t) -> p l t", t=4),
+                in0=g_src,
+                in1=g_src,
+                op=ALU.mult,
+            )
+            cols = slice(h * HALF, (h + 1) * HALF)
+            nc.vector.quantize_mx(
+                out=x_codes[b][:, cp, cols].bitcast(FP8X4),
+                scales=x_scales[b][:, cp, cols],
+                in_=shared[:, 4 * base : 4 * (base + HALF)],
+            )
+
         def normalise(b, cj, split):
             oview = out[b].rearrange("(c p j) l -> c j p l", c=2, j=4)[cj // 4, cj % 4]
             r = rpool.tile([P, L], F32, name="r")
             o = opool.tile([P, L], F32, name="o")
+            xin = xs[b][:, cj, :]
+            if b < PSUM_X_BATCHES:
+                xp = psum.tile([P, L], BF16, name="xp", tag="bank")
+                for h in range(2):
+                    cols = slice(h * HALF, (h + 1) * HALF)
+                    nc.tensor.matmul(out=xp[:, cols], lhsT=ident_bf[:], rhs=xs[b][:, cj, cols], start=True, stop=True)
+                xin = xp[:]
             for h in range(2):
                 cols = slice(h * HALF, (h + 1) * HALF)
                 acc = psum.tile([P, HALF], F32, name="acc", tag="bank")
@@ -142,10 +181,10 @@ def tile_gdn_1d_t_kernel(tc, x, beta_param, gamma_param, out):
                     out=r[:, cols], in_=acc[:], func=ACT.Abs_reciprocal_sqrt, bias=beta[:, cj : cj + 1], scale=1.0
                 )
                 if split:
-                    nc.vector.tensor_tensor(out=o[:, cols], in0=xs[b][:, cj, cols], in1=r[:, cols], op=ALU.mult)
+                    nc.vector.tensor_tensor(out=o[:, cols], in0=xin[:, cols], in1=r[:, cols], op=ALU.mult)
                     nc.sync.dma_start(out=oview[:, cols], in_=o[:, cols])
             if not split:
-                nc.vector.tensor_tensor(out=o[:], in0=xs[b][:, cj, :], in1=r[:], op=ALU.mult)
+                nc.vector.tensor_tensor(out=o[:], in0=xin, in1=r[:], op=ALU.mult)
                 nc.sync.dma_start(out=oview, in_=o[:])
 
         units = [(cp, h) for h in range(2) for cp in range(2)]
@@ -157,6 +196,6 @@ def tile_gdn_1d_t_kernel(tc, x, beta_param, gamma_param, out):
         for b in range(B):
             for g in range(4):
                 if b + 1 < B:
-                    square_and_quantise(b + 1, units[g][0], units[g][1])
+                    square_shared(4 * b + g, b + 1, units[g][0], units[g][1])
                 for cj in (2 * g, 2 * g + 1):
                     normalise(b, cj, 8 * b + cj >= 8 * B - SPLIT_ROWS)

@@ -19,7 +19,11 @@ PEDESTAL = 2.0 ** -36
 BETA_BOUND = (1e-06 + PEDESTAL) ** 0.5
 WS = 320
 SPLIT_ROWS = 2
-SA = 256
+SA = 216
+VC = 96
+GM = HALF - SA - VC
+W = SA + VC
+UNITS = 12
 PSUM_X_BATCHES = 3
 
 FLOPS = 2 * B * C * C * L
@@ -32,9 +36,10 @@ def tile_gdn_1d_t_kernel(tc, x, beta_param, gamma_param, out):
         sqf = ctx.enter_context(tc.tile_pool(name="sqf", bufs=2))
         gbf = ctx.enter_context(tc.tile_pool(name="gbf", bufs=2))
         sqpool = ctx.enter_context(tc.tile_pool(name="sqpool", bufs=3))
-        rpool = ctx.enter_context(tc.tile_pool(name="rpool", bufs=3))
+        rpool = ctx.enter_context(tc.tile_pool(name="rpool", bufs=4))
         opool = ctx.enter_context(tc.tile_pool(name="opool", bufs=4))
-        psum = ctx.enter_context(tc.psum_pool(name="psum", bufs=8))
+        psum = ctx.enter_context(tc.psum_pool(name="psum", bufs=5))
+        psum_x = ctx.enter_context(tc.psum_pool(name="psum_x", bufs=3))
 
         one = keep.tile([P, 1], F32, name="one")
         nc.vector.memset(one[:], 1.0)
@@ -79,6 +84,8 @@ def tile_gdn_1d_t_kernel(tc, x, beta_param, gamma_param, out):
         g_codes = keep.tile([P, 2048], U32, name="g_codes", align_bytes=64)
         g_scales = keep.tile([P, 2048], U8, name="g_scales", align_bytes=64)
 
+        shared = keep.tile([P, (HALF + W) * 4], BF16, name="shared", align_bytes=64)
+
         def gamma_unit(q):
             t = keep.tile([P, 2 * C], BF16, name="t%d" % q)
             nc.vector.tensor_scalar_max(out=t[:], in0=gp[q][:].rearrange("p g i -> p (g i)"), scalar1=A)
@@ -99,12 +106,16 @@ def tile_gdn_1d_t_kernel(tc, x, beta_param, gamma_param, out):
                         in_=bank_bf[:, cp * 512 : (cp + 1) * 512].rearrange("q (u m e) -> q m u e", u=2, e=2),
                         func=ACT.Square,
                     )
-            gb = gbf.tile([P, 2048], BF16, name="gb", align_bytes=64)
-            nc.vector.tensor_scalar_add(out=gb[:], in0=sq[:].rearrange("q g c n -> q (g c n)"), scalar1=-PEDESTAL)
+            if q < 3:
+                gbt = gbf.tile([P, 2048], BF16, name="gb", align_bytes=64)
+                gb = gbt[:]
+            else:
+                gb = shared[:, 4 * W : 4 * (W + HALF)]
+            nc.vector.tensor_scalar_add(out=gb, in0=sq[:].rearrange("q g c n -> q (g c n)"), scalar1=-PEDESTAL)
             nc.vector.quantize_mx(
                 out=g_codes[:, q * 512 : (q + 1) * 512].bitcast(FP8X4),
                 scales=g_scales[:, q * 512 : (q + 1) * 512],
-                in_=gb[:],
+                in_=gb,
             )
 
         x_codes = [keep.tile([P, 2, L], U32, name="xc%d" % b, align_bytes=64) for b in range(B)]
@@ -124,31 +135,37 @@ def tile_gdn_1d_t_kernel(tc, x, beta_param, gamma_param, out):
                 in_=xg[:].rearrange("p w t -> p (w t)"),
             )
 
-        GM = HALF - SA
-        shared = keep.tile([P, (2 * SA + GM) * 4], BF16, name="shared", align_bytes=64)
+        def unit_rows(n):
+            cp, h = units[n % 4]
+            return xs[1 + n // 4][:, 4 * cp : 4 * cp + 4, h * HALF : (h + 1) * HALF]
 
-        def square_shared(n, b, cp, h):
-            if n % 2 == 0:
-                base, s_tile, g_tile, s_pos, g_pos = 0, 0, SA, 0, SA
-            else:
-                base, s_tile, g_tile, s_pos, g_pos = SA, SA + GM, SA, GM, 0
-            rows = xs[b][:, 4 * cp : 4 * cp + 4, h * HALF : (h + 1) * HALF]
-            nc.scalar.activation(
-                out=shared[:, 4 * s_tile : 4 * (s_tile + SA)].rearrange("p (c i t) -> p c t i", i=4, t=4),
-                in_=rows[:, :, s_pos : s_pos + SA].rearrange("p t (c i) -> p c t i", i=4),
-                func=ACT.Square,
-            )
-            g_src = rows[:, :, g_pos : g_pos + GM].rearrange("p t l -> p l t")
+        def blocked(n, tile_pos, pos, count):
+            dst = shared[:, 4 * tile_pos : 4 * (tile_pos + count)].rearrange("p (c i t) -> p c t i", i=4, t=4)
+            src = unit_rows(n)[:, :, pos : pos + count].rearrange("p t (c i) -> p c t i", i=4)
+            return dst, src
+
+        def square_scalar(n):
+            dst, src = blocked(n, 0, 0, SA) if n % 2 == 0 else blocked(n, HALF + VC, GM + VC, SA)
+            nc.scalar.activation(out=dst, in_=src, func=ACT.Square)
+
+        def square_vector(n):
+            dst, src = blocked(n, SA, SA, VC) if n % 2 == 0 else blocked(n, HALF, GM, VC)
+            nc.vector.tensor_tensor(out=dst, in0=src, in1=src, op=ALU.mult)
+
+        def square_gpsimd(n):
+            pos = W if n % 2 == 0 else 0
+            src = unit_rows(n)[:, :, pos : pos + GM].rearrange("p t l -> p l t")
             nc.gpsimd.tensor_tensor(
-                out=shared[:, 4 * g_tile : 4 * (g_tile + GM)].rearrange("p (l t) -> p l t", t=4),
-                in0=g_src,
-                in1=g_src,
-                op=ALU.mult,
+                out=shared[:, 4 * W : 4 * HALF].rearrange("p (l t) -> p l t", t=4), in0=src, in1=src, op=ALU.mult
             )
+
+        def quantise_unit(n):
+            cp, h = units[n % 4]
             cols = slice(h * HALF, (h + 1) * HALF)
+            base = 0 if n % 2 == 0 else W
             nc.vector.quantize_mx(
-                out=x_codes[b][:, cp, cols].bitcast(FP8X4),
-                scales=x_scales[b][:, cp, cols],
+                out=x_codes[1 + n // 4][:, cp, cols].bitcast(FP8X4),
+                scales=x_scales[1 + n // 4][:, cp, cols],
                 in_=shared[:, 4 * base : 4 * (base + HALF)],
             )
 
@@ -158,7 +175,7 @@ def tile_gdn_1d_t_kernel(tc, x, beta_param, gamma_param, out):
             o = opool.tile([P, L], F32, name="o")
             xin = xs[b][:, cj, :]
             if b < PSUM_X_BATCHES:
-                xp = psum.tile([P, L], BF16, name="xp", tag="bank")
+                xp = psum_x.tile([P, L], BF16, name="xp")
                 for h in range(2):
                     cols = slice(h * HALF, (h + 1) * HALF)
                     nc.tensor.matmul(out=xp[:, cols], lhsT=ident_bf[:], rhs=xs[b][:, cj, cols], start=True, stop=True)
@@ -191,11 +208,22 @@ def tile_gdn_1d_t_kernel(tc, x, beta_param, gamma_param, out):
         gamma_unit(0)
         for cp, h in units:
             square_and_quantise(0, cp, h)
-        for q in range(1, 4):
+        for q in range(1, 3):
             gamma_unit(q)
-        for b in range(B):
-            for g in range(4):
-                if b + 1 < B:
-                    square_shared(4 * b + g, b + 1, units[g][0], units[g][1])
-                for cj in (2 * g, 2 * g + 1):
-                    normalise(b, cj, 8 * b + cj >= 8 * B - SPLIT_ROWS)
+        square_scalar(0)
+        square_vector(0)
+        gamma_unit(3)
+        square_gpsimd(0)
+        with tc.manual_schedule(engines={mybir.EngineType.DVE}):
+            for b in range(B):
+                for g in range(4):
+                    n = 4 * b + g
+                    if n + 1 < UNITS:
+                        square_scalar(n + 1)
+                        square_vector(n + 1)
+                    if n < UNITS:
+                        quantise_unit(n)
+                    if n + 1 < UNITS:
+                        square_gpsimd(n + 1)
+                    for cj in (2 * g, 2 * g + 1):
+                        normalise(b, cj, 8 * b + cj >= 8 * B - SPLIT_ROWS)

@@ -110,7 +110,7 @@ def tile_gdn_1d_t_kernel(tc, x, beta_param, gamma_param, out):
                 gbt = gbf.tile([P, 2048], BF16, name="gb", align_bytes=64)
                 gb = gbt[:]
             else:
-                gb = shared[:, 4 * W : 4 * (W + HALF)]
+                gb = shared[:, : 4 * HALF]
             nc.vector.tensor_scalar_add(out=gb, in0=sq[:].rearrange("q g c n -> q (g c n)"), scalar1=-PEDESTAL)
             nc.vector.quantize_mx(
                 out=g_codes[:, q * 512 : (q + 1) * 512].bitcast(FP8X4),
@@ -210,20 +210,21 @@ def tile_gdn_1d_t_kernel(tc, x, beta_param, gamma_param, out):
             square_and_quantise(0, cp, h)
         for q in range(1, 3):
             gamma_unit(q)
-        square_scalar(0)
-        square_vector(0)
-        gamma_unit(3)
-        square_gpsimd(0)
+        square_and_quantise(1, units[0][0], units[0][1])
+        square_scalar(1)
         with tc.manual_schedule(engines={mybir.EngineType.DVE}):
+            square_vector(1)
+            gamma_unit(3)
+            square_gpsimd(1)
             for b in range(B):
                 for g in range(4):
                     n = 4 * b + g
-                    if n + 1 < UNITS:
-                        square_scalar(n + 1)
-                        square_vector(n + 1)
-                    if n < UNITS:
+                    if 1 <= n < UNITS:
+                        if n + 1 < UNITS:
+                            square_scalar(n + 1)
+                            square_vector(n + 1)
                         quantise_unit(n)
-                    if n + 1 < UNITS:
-                        square_gpsimd(n + 1)
+                        if n + 1 < UNITS:
+                            square_gpsimd(n + 1)
                     for cj in (2 * g, 2 * g + 1):
                         normalise(b, cj, 8 * b + cj >= 8 * B - SPLIT_ROWS)

@@ -36,8 +36,8 @@ def tile_gdn_1d_t_kernel(tc, x, beta_param, gamma_param, out):
         sqf = ctx.enter_context(tc.tile_pool(name="sqf", bufs=2))
         gbf = ctx.enter_context(tc.tile_pool(name="gbf", bufs=2))
         sqpool = ctx.enter_context(tc.tile_pool(name="sqpool", bufs=3))
-        rpool = ctx.enter_context(tc.tile_pool(name="rpool", bufs=4))
-        opool = ctx.enter_context(tc.tile_pool(name="opool", bufs=4))
+        rpool = ctx.enter_context(tc.tile_pool(name="rpool", bufs=5))
+        opool = ctx.enter_context(tc.tile_pool(name="opool", bufs=6))
         psum = ctx.enter_context(tc.psum_pool(name="psum", bufs=5))
         psum_x = ctx.enter_context(tc.psum_pool(name="psum_x", bufs=3))
 

@@ -97,15 +97,13 @@ def tile_gdn_1d_t_kernel(tc, x, beta_param, gamma_param, out):
                     w0 = g * 512 + 256 * cp
                     words = tw[:, w0 : w0 + 256].rearrange("p (q u) -> p u q", u=2)
                     for u in range(2):
-                        col = (2 * cp + u) * P
+                        col = (2 * u + cp) * P
                         nc.tensor.transpose(bank[:, col : col + P], words[:, u, :], ident[:])
-                bank_bf = bank[:].bitcast(BF16)
-                for cp in range(2):
-                    nc.scalar.activation(
-                        out=sq[:, g, cp, :].rearrange("q (m u e) -> q m u e", u=2, e=2),
-                        in_=bank_bf[:, cp * 512 : (cp + 1) * 512].rearrange("q (u m e) -> q m u e", u=2, e=2),
-                        func=ACT.Square,
-                    )
+                nc.scalar.activation(
+                    out=sq[:, g].rearrange("q c (m u e) -> q (c m) u e", u=2, e=2),
+                    in_=bank[:].bitcast(BF16).rearrange("q (u m e) -> q m u e", u=2, e=2),
+                    func=ACT.Square,
+                )
             if q < 3:
                 gbt = gbf.tile([P, 2048], BF16, name="gb", align_bytes=64)
                 gb = gbt[:]

@@ -104,16 +104,12 @@ def tile_gdn_1d_t_kernel(tc, x, beta_param, gamma_param, out):
                     in_=bank[:].bitcast(BF16).rearrange("q (u m e) -> q m u e", u=2, e=2),
                     func=ACT.Square,
                 )
-            if q < 3:
-                gbt = gbf.tile([P, 2048], BF16, name="gb", align_bytes=64)
-                gb = gbt[:]
-            else:
-                gb = shared[:, : 4 * HALF]
-            nc.vector.tensor_scalar_add(out=gb, in0=sq[:].rearrange("q g c n -> q (g c n)"), scalar1=-PEDESTAL)
+            gb = gbf.tile([P, 2048], BF16, name="gb", align_bytes=64)
+            nc.vector.tensor_scalar_add(out=gb[:], in0=sq[:].rearrange("q g c n -> q (g c n)"), scalar1=-PEDESTAL)
             nc.vector.quantize_mx(
                 out=g_codes[:, q * 512 : (q + 1) * 512].bitcast(FP8X4),
                 scales=g_scales[:, q * 512 : (q + 1) * 512],
-                in_=gb,
+                in_=gb[:],
             )
 
         x_codes = [keep.tile([P, 2, L], U32, name="xc%d" % b, align_bytes=64) for b in range(B)]
@@ -206,13 +202,16 @@ def tile_gdn_1d_t_kernel(tc, x, beta_param, gamma_param, out):
         gamma_unit(0)
         for cp, h in units:
             square_and_quantise(0, cp, h)
-        for q in range(1, 3):
+        for q in range(1, 4):
             gamma_unit(q)
-        square_and_quantise(1, units[0][0], units[0][1])
+        dst, src = blocked(0, 0, 0, WS)
+        nc.scalar.activation(out=dst, in_=src, func=ACT.Square)
         square_scalar(1)
         with tc.manual_schedule(engines={mybir.EngineType.DVE}):
+            dst, src = blocked(0, WS, WS, HALF - WS)
+            nc.vector.tensor_tensor(out=dst, in0=src, in1=src, op=ALU.mult)
             square_vector(1)
-            gamma_unit(3)
+            quantise_unit(0)
             square_gpsimd(1)
             for b in range(B):
                 for g in range(4):

from contextlib import ExitStack

import concourse.mybir as mybir
from concourse.masks import make_identity

F32 = mybir.dt.float32
BF16 = mybir.dt.bfloat16
U32 = mybir.dt.uint32
U8 = mybir.dt.uint8
FP8X4 = mybir.dt.float8_e4m3fn_x4
ACT = mybir.ActivationFunctionType
ALU = mybir.AluOpType

P = 128
B, C, L = 4, 1024, 1024
HALF = 512
A = 2.0 ** -18
PEDESTAL = 2.0 ** -36
BETA_BOUND = (1e-06 + PEDESTAL) ** 0.5
WS = 320
SPLIT_ROWS = 2
SA = 216
VC = 96
GM = HALF - SA - VC
W = SA + VC
UNITS = 12
PSUM_X_BATCHES = 3

FLOPS = 2 * B * C * C * L


def tile_gdn_1d_t_kernel(tc, x, beta_param, gamma_param, out):
    nc = tc.nc
    with ExitStack() as ctx:
        keep = ctx.enter_context(tc.tile_pool(name="keep", bufs=1))
        sqf = ctx.enter_context(tc.tile_pool(name="sqf", bufs=2))
        gbf = ctx.enter_context(tc.tile_pool(name="gbf", bufs=2))
        sqpool = ctx.enter_context(tc.tile_pool(name="sqpool", bufs=3))
        rpool = ctx.enter_context(tc.tile_pool(name="rpool", bufs=5))
        opool = ctx.enter_context(tc.tile_pool(name="opool", bufs=6))
        psum = ctx.enter_context(tc.psum_pool(name="psum", bufs=5))
        psum_x = ctx.enter_context(tc.psum_pool(name="psum_x", bufs=3))

        one = keep.tile([P, 1], F32, name="one")
        nc.vector.memset(one[:], 1.0)
        warm = keep.tile([P, 1], F32, name="warm")
        nc.scalar.activation(out=warm[:], in_=one[:], func=ACT.Abs_reciprocal_sqrt)

        ident = keep.tile([P, P], F32, name="ident")
        make_identity(nc, ident[:])
        ident_bf = keep.tile([P, P], BF16, name="ident_bf")
        make_identity(nc, ident_bf[:])

        bp = keep.tile([P, 2, 4], BF16, name="bp")
        nc.scalar.dma_start(out=bp[:], in_=beta_param.rearrange("(c p j) -> p c j", c=2, j=4))
        gview = gamma_param.rearrange("(c p j) i -> c p j i", c=2, j=4)
        gp = [keep.tile([P, 2, C], BF16, name="gp%d" % q) for q in range(4)]
        xs = [keep.tile([P, 8, L], BF16, name="x%d" % b) for b in range(B)]

        def load_gamma(q):
            j0 = 2 * (q % 2)
            nc.sync.dma_start(out=gp[q][:], in_=gview[q // 2][:, j0 : j0 + 2, :])

        def load_x(b, c):
            xview = x[b].rearrange("(c p j) l -> c p j l", c=2, j=4)
            nc.sync.dma_start(out=xs[b][:, 4 * c : 4 * c + 4, :], in_=xview[c])

        load_gamma(0)
        load_x(0, 0)
        load_x(0, 1)
        for q in range(1, 4):
            load_gamma(q)
        for b in range(1, B):
            load_x(b, 0)
            load_x(b, 1)

        bt = keep.tile([P, 8], F32, name="bt")
        nc.vector.tensor_scalar_max(out=bt[:], in0=bp[:].rearrange("p c j -> p (c j)"), scalar1=BETA_BOUND)
        bsq = keep.tile([P, 8], F32, name="bsq")
        nc.vector.tensor_tensor(out=bsq[:], in0=bt[:], in1=bt[:], op=ALU.mult)
        beta = keep.tile([P, 8], F32, name="beta")
        nc.vector.tensor_scalar_add(out=beta[:], in0=bsq[:], scalar1=-PEDESTAL)

        g_codes = keep.tile([P, 2048], U32, name="g_codes", align_bytes=64)
        g_scales = keep.tile([P, 2048], U8, name="g_scales", align_bytes=64)

        shared = keep.tile([P, (HALF + W) * 4], BF16, name="shared", align_bytes=64)

        def gamma_unit(q):
            t = keep.tile([P, 2 * C], BF16, name="t%d" % q)
            nc.vector.tensor_scalar_max(out=t[:], in0=gp[q][:].rearrange("p g i -> p (g i)"), scalar1=A)
            tw = t[:].bitcast(F32)
            sq = sqf.tile([P, 2, 2, 512], F32, name="sq")
            for g in range(2):
                bank = psum.tile([P, HALF], F32, name="bank", tag="bank")
                for cp in range(2):
                    w0 = g * 512 + 256 * cp
                    words = tw[:, w0 : w0 + 256].rearrange("p (q u) -> p u q", u=2)
                    for u in range(2):
                        col = (2 * u + cp) * P
                        nc.tensor.transpose(bank[:, col : col + P], words[:, u, :], ident[:])
                nc.scalar.activation(
                    out=sq[:, g].rearrange("q c (m u e) -> q (c m) u e", u=2, e=2),
                    in_=bank[:].bitcast(BF16).rearrange("q (u m e) -> q m u e", u=2, e=2),
                    func=ACT.Square,
                )
            gb = gbf.tile([P, 2048], BF16, name="gb", align_bytes=64)
            nc.vector.tensor_scalar_add(out=gb[:], in0=sq[:].rearrange("q g c n -> q (g c n)"), scalar1=-PEDESTAL)
            nc.vector.quantize_mx(
                out=g_codes[:, q * 512 : (q + 1) * 512].bitcast(FP8X4),
                scales=g_scales[:, q * 512 : (q + 1) * 512],
                in_=gb[:],
            )

        x_codes = [keep.tile([P, 2, L], U32, name="xc%d" % b, align_bytes=64) for b in range(B)]
        x_scales = [keep.tile([P, 2, L], U8, name="xsc%d" % b, align_bytes=64) for b in range(B)]

        def square_and_quantise(b, cp, h):
            cols = slice(h * HALF, (h + 1) * HALF)
            xg = sqpool.tile([P, HALF, 4], BF16, name="xg", align_bytes=64)
            src = xs[b][:, 4 * cp : 4 * cp + 4, cols].rearrange("p t (c i) -> p c t i", i=4)
            dst = xg[:].rearrange("p (c i) t -> p c t i", i=4)
            cs = WS // 4
            nc.scalar.activation(out=dst[:, :cs], in_=src[:, :cs], func=ACT.Square)
            nc.vector.tensor_tensor(out=dst[:, cs:], in0=src[:, cs:], in1=src[:, cs:], op=ALU.mult)
            nc.vector.quantize_mx(
                out=x_codes[b][:, cp, cols].bitcast(FP8X4),
                scales=x_scales[b][:, cp, cols],
                in_=xg[:].rearrange("p w t -> p (w t)"),
            )

        def unit_rows(n):
            cp, h = units[n % 4]
            return xs[1 + n // 4][:, 4 * cp : 4 * cp + 4, h * HALF : (h + 1) * HALF]

        def blocked(n, tile_pos, pos, count):
            dst = shared[:, 4 * tile_pos : 4 * (tile_pos + count)].rearrange("p (c i t) -> p c t i", i=4, t=4)
            src = unit_rows(n)[:, :, pos : pos + count].rearrange("p t (c i) -> p c t i", i=4)
            return dst, src

        def square_scalar(n):
            dst, src = blocked(n, 0, 0, SA) if n % 2 == 0 else blocked(n, HALF + VC, GM + VC, SA)
            nc.scalar.activation(out=dst, in_=src, func=ACT.Square)

        def square_vector(n):
            dst, src = blocked(n, SA, SA, VC) if n % 2 == 0 else blocked(n, HALF, GM, VC)
            nc.vector.tensor_tensor(out=dst, in0=src, in1=src, op=ALU.mult)

        def square_gpsimd(n):
            pos = W if n % 2 == 0 else 0
            src = unit_rows(n)[:, :, pos : pos + GM].rearrange("p t l -> p l t")
            nc.gpsimd.tensor_tensor(
                out=shared[:, 4 * W : 4 * HALF].rearrange("p (l t) -> p l t", t=4), in0=src, in1=src, op=ALU.mult
            )

        def quantise_unit(n):
            cp, h = units[n % 4]
            cols = slice(h * HALF, (h + 1) * HALF)
            base = 0 if n % 2 == 0 else W
            nc.vector.quantize_mx(
                out=x_codes[1 + n // 4][:, cp, cols].bitcast(FP8X4),
                scales=x_scales[1 + n // 4][:, cp, cols],
                in_=shared[:, 4 * base : 4 * (base + HALF)],
            )

        def normalise(b, cj, split):
            oview = out[b].rearrange("(c p j) l -> c j p l", c=2, j=4)[cj // 4, cj % 4]
            r = rpool.tile([P, L], F32, name="r")
            o = opool.tile([P, L], F32, name="o")
            xin = xs[b][:, cj, :]
            if b < PSUM_X_BATCHES:
                xp = psum_x.tile([P, L], BF16, name="xp")
                for h in range(2):
                    cols = slice(h * HALF, (h + 1) * HALF)
                    nc.tensor.matmul(out=xp[:, cols], lhsT=ident_bf[:], rhs=xs[b][:, cj, cols], start=True, stop=True)
                xin = xp[:]
            for h in range(2):
                cols = slice(h * HALF, (h + 1) * HALF)
                acc = psum.tile([P, HALF], F32, name="acc", tag="bank")
                for cp in range(2):
                    w0 = cj * 256 + cp * P
                    nc.tensor.matmul_mx(
                        out=acc[:],
                        lhsT=g_codes[:, w0 : w0 + P].bitcast(FP8X4),
                        lhsT_scale=g_scales[:, w0 : w0 + P],
                        rhs=x_codes[b][:, cp, cols].bitcast(FP8X4),
                        rhs_scale=x_scales[b][:, cp, cols],
                        start=(cp == 0),
                        stop=(cp == 1),
                    )
                nc.scalar.activation(
                    out=r[:, cols], in_=acc[:], func=ACT.Abs_reciprocal_sqrt, bias=beta[:, cj : cj + 1], scale=1.0
                )
                if split:
                    nc.vector.tensor_tensor(out=o[:, cols], in0=xin[:, cols], in1=r[:, cols], op=ALU.mult)
                    nc.sync.dma_start(out=oview[:, cols], in_=o[:, cols])
            if not split:
                nc.vector.tensor_tensor(out=o[:], in0=xin, in1=r[:], op=ALU.mult)
                nc.sync.dma_start(out=oview, in_=o[:])

        units = [(cp, h) for h in range(2) for cp in range(2)]
        gamma_unit(0)
        for cp, h in units:
            square_and_quantise(0, cp, h)
        for q in range(1, 4):
            gamma_unit(q)
        dst, src = blocked(0, 0, 0, WS)
        nc.scalar.activation(out=dst, in_=src, func=ACT.Square)
        square_scalar(1)
        with tc.manual_schedule(engines={mybir.EngineType.DVE}):
            dst, src = blocked(0, WS, WS, HALF - WS)
            nc.vector.tensor_tensor(out=dst, in0=src, in1=src, op=ALU.mult)
            square_vector(1)
            quantise_unit(0)
            square_gpsimd(1)
            for b in range(B):
                for g in range(4):
                    n = 4 * b + g
                    if 1 <= n < UNITS:
                        if n + 1 < UNITS:
                            square_scalar(n + 1)
                            square_vector(n + 1)
                        quantise_unit(n)
                        if n + 1 < UNITS:
                            square_gpsimd(n + 1)
                    for cj in (2 * g, 2 * g + 1):
                        normalise(b, cj, 8 * b + cj >= 8 * B - SPLIT_ROWS)
